import numpy as np
import ml_dtypes


def mxq(x, axis, fmt="e4m3"):
    dtype, down = {"e4m3": (ml_dtypes.float8_e4m3fn, 7), "e5m2": (ml_dtypes.float8_e5m2, 14)}[fmt]
    v = np.moveaxis(np.asarray(x, np.float32).astype(ml_dtypes.bfloat16).astype(np.float64), axis, -1)
    blocks = v.reshape(v.shape[:-1] + (-1, 32))
    amax = np.abs(blocks).max(-1, keepdims=True)
    byte = np.maximum(np.where(amax > 0, np.frexp(amax)[1] - 1 + 127, 0) - down, 1)
    scale = np.exp2(byte - 127.0)
    codes = (blocks / scale).astype(np.float32).astype(dtype).astype(np.float64)
    return np.moveaxis((codes * scale).reshape(v.shape), -1, axis)


WIDE = False


def mx_kscale(k):
    if not WIDE:
        return np.ones(k)
    levels = np.array([10, -10, 5, -5, 0])
    a = np.random.permutation(np.resize(levels, k // 512 * 4)).reshape(k // 512, 4)
    idx = np.arange(k)
    return np.exp2(a[idx // 512, idx % 128 // 32])


BF16 = ml_dtypes.bfloat16


def bf(x):
    return np.asarray(x, np.float32).astype(BF16)


def f64(x):
    return np.asarray(x).astype(np.float64)


B, S, D, DV, DK = 1, 1024, 1024, 1024, 256
DROPOUT_P = 0.1
KEEP = 1.0 - DROPOUT_P


def setup_inputs():
    s = mx_kscale(D)
    return {
        "q": bf(np.random.standard_normal((B, S, DK)) * 2.0 / DK ** 0.25),
        "k": bf(np.random.standard_normal((B, S, DK)) * 2.0 / DK ** 0.25),
        "x3": bf(np.random.standard_normal((B, S, D)) * s),
        "Wv": bf(np.random.standard_normal((DV, D)) / np.sqrt(D) / s),
        "bv": bf(np.random.standard_normal(DV) * 0.1),
        "inv_scale": bf(np.random.uniform(size=(S, S)) + 1.0),
        "dropout_mask": bf((np.random.uniform(size=(B, S, S)) < KEEP) / KEEP),
    }


def reference(q, k, x3, Wv, bv, inv_scale, dropout_mask):
    v = (mxq(f64(x3), 2, "e4m3") @ mxq(f64(Wv), 1, "e4m3").T) + f64(bv)
    attn = f64(q) @ f64(k).transpose(0, 2, 1)
    scaled = attn / f64(inv_scale)
    e = np.exp(scaled - scaled.max(-1, keepdims=True))
    pe = e * f64(dropout_mask)
    return (mxq(pe, 2, "e4m3") @ mxq(v, 1, "e4m3")) / e.sum(-1, keepdims=True)

@@ -1,0 +1,379 @@
+from contextlib import ExitStack
+
+import concourse.mybir as mybir
+from concourse.masks import make_identity
+
+F32 = mybir.dt.float32
+BF16 = mybir.dt.bfloat16
+I32 = mybir.dt.int32
+U32 = mybir.dt.uint32
+U8 = mybir.dt.uint8
+FP8X4 = mybir.dt.float8_e4m3fn_x4
+ALU = mybir.AluOpType
+ACT = mybir.ActivationFunctionType
+AXIS = mybir.AxisListType
+
+P = 128
+PACK = 4
+K_PASS = P * PACK
+S = 1024
+D = 1024
+DV = 1024
+DK = 256
+BANK = 512
+
+TILES = S // P
+PAIRS = TILES // 2
+PASSES = S // K_PASS
+DK_HALVES = DK // P
+DV_HALVES = DV // BANK
+PAIR_COLS = PASSES * 2 * P
+
+FLOPS = 2 * S * D * DV + 2 * S * S * DK + 2 * S * S * DV
+
+
+def tile_model_pa_kernel(tc, q, k, x3, Wv, bv, inv_scale, dropout_mask, out):
+    nc = tc.nc
+    with ExitStack() as ctx:
+        ctx.enter_context(tc.manual_schedule())
+        keep = ctx.enter_context(tc.tile_pool(name="keep", bufs=1))
+        stream = ctx.enter_context(tc.tile_pool(name="stream", bufs=2))
+        small = ctx.enter_context(tc.tile_pool(name="small", bufs=6))
+        psum = ctx.enter_context(tc.psum_pool(name="psum", bufs=2))
+
+        x3_rows = x3.flatten_outer_dims().rearrange("(a p e) d -> a p (e d)", p=P, e=2)
+        wv_rows = Wv.rearrange("(a t p) d -> a p t d", t=2, p=P)
+        inv_rows = inv_scale.rearrange("(p a i) n -> a p (i n)", a=PAIRS, i=2)
+        mask_rows = dropout_mask.flatten_outer_dims().rearrange(
+            "(p a i) n -> a p (i n)", a=PAIRS, i=2
+        )
+        out_rows = out.flatten_outer_dims().rearrange("(p i) n -> i p n", i=TILES)
+
+        bias_row = keep.tile([P, DV], BF16)
+        nc.vector.memset(bias_row[:].bitcast(I32), 0)
+        nc.sync.dma_start(out=bias_row[0:1, :], in_=bv.rearrange("(o n) -> o n", o=1))
+        inv_sb = []
+        x3_sb = []
+        for a in range(PAIRS):
+            inv_sb.append(keep.tile([P, 2 * S], BF16, name="inv%d" % a))
+            nc.sync.dma_start(out=inv_sb[a][:], in_=inv_rows[a])
+            x3_sb.append(keep.tile([P, 2 * D], BF16, name="x3_%d" % a))
+            nc.sync.dma_start(out=x3_sb[a][:], in_=x3_rows[a])
+        wv_sb = []
+        for a in range(PAIRS):
+            wv_sb.append(keep.tile([P, 2 * D], BF16, name="wv_%d" % a))
+            nc.sync.dma_start(
+                out=wv_sb[a][:].rearrange("p (t d) -> p t d", t=2), in_=wv_rows[a]
+            )
+        k_sb = keep.tile([P, TILES * DK], BF16)
+        nc.sync.dma_start(
+            out=k_sb[:].rearrange("p (t d) -> p t d", t=TILES),
+            in_=k.flatten_outer_dims().rearrange("(t p) d -> p t d", p=P),
+        )
+        q_sb = keep.tile([P, TILES * DK], BF16)
+        nc.sync.dma_start(
+            out=q_sb[:], in_=q.flatten_outer_dims().rearrange("(p i) d -> p (i d)", i=TILES)
+        )
+        mask_sb = []
+        for a in range(PAIRS):
+            mask_sb.append(keep.tile([P, 2 * S], BF16, name="mask%d" % a))
+            nc.sync.dma_start(out=mask_sb[a][:], in_=mask_rows[a])
+
+        def query_tile(pair_list, i):
+            return pair_list[i // 2][:, (i % 2) * S : (i % 2 + 1) * S]
+
+        ident_f32 = keep.tile([P, P], F32)
+        make_identity(nc, ident_f32[:])
+        ident_bf16 = keep.tile([P, P], BF16)
+        make_identity(nc, ident_bf16[:])
+        ones = keep.tile([P, P], BF16)
+        nc.vector.memset(ones[:], 1.0)
+        bias_sb = keep.tile([P, DV], BF16)
+        for half in range(DV_HALVES):
+            cols = slice(half * BANK, (half + 1) * BANK)
+            spread = psum.tile([P, BANK], F32, tag="turn")
+            nc.tensor.matmul(out=spread[:], lhsT=ones[:], rhs=bias_row[:, cols], start=True, stop=True)
+            nc.vector.tensor_copy(out=bias_sb[:, cols], in_=spread[:])
+
+        recip = []
+        x_times_seed = {}
+
+        def logarithm(a):
+            recip.append(keep.tile([P, 2 * S], F32, name="recip%d" % a))
+            nc.scalar.activation(out=recip[a][:], in_=inv_sb[a][:], func=ACT.Ln)
+
+        def seed(i):
+            r = query_tile(recip, i)
+            nc.scalar.activation(out=r, in_=r, func=ACT.Exp, scale=-1.0)
+            x_times_seed[i] = stream.tile([P, S], F32, name="x_times_seed", bufs=4)
+            nc.gpsimd.tensor_tensor(
+                out=x_times_seed[i][:], in0=query_tile(inv_sb, i), in1=r, op=ALU.mult
+            )
+
+        def newton(i):
+            r = query_tile(recip, i)
+            nc.vector.scalar_tensor_tensor(
+                out=r, in0=x_times_seed[i][:], scalar=2.0, in1=r, op0=ALU.subtract, op1=ALU.mult
+            )
+
+        x3_codes = keep.tile([P, PAIRS, PAIR_COLS], U32, align_bytes=64)
+        x3_scales = keep.tile([P, PAIRS, PAIR_COLS], U8, align_bytes=64)
+        wv_codes = keep.tile([P, PAIRS, PAIR_COLS], U32, align_bytes=64)
+        wv_scales = keep.tile([P, PAIRS, PAIR_COLS], U8, align_bytes=64)
+        row_pairs = [(x3_sb[a], x3_codes[:, a, :], x3_scales[:, a, :]) for a in range(PAIRS)] + [
+            (wv_sb[a], wv_codes[:, a, :], wv_scales[:, a, :]) for a in range(PAIRS)
+        ]
+        turned_rows = {}
+        grouped_rows = {}
+
+        def turn_rows(n):
+            words = row_pairs[n][0][:].bitcast(F32)
+            for t in range(2):
+                turned = psum.tile([P, PASSES, 2, P], F32, tag="wide", bufs=4)
+                for c in range(PASSES):
+                    for u in range(2):
+                        first = ((t * PASSES + c) * 2 + u) * P
+                        nc.tensor.transpose(
+                            out=turned[:, c, u, :],
+                            in_=words[:, first : first + P],
+                            identity=ident_f32[:],
+                        )
+                turned_rows[n, t] = turned
+
+        def gather_rows(n):
+            grouped = stream.tile([P, PAIR_COLS * PACK], BF16, align_bytes=64, bufs=3)
+            grouped_words = grouped[:].bitcast(F32).rearrange(
+                "p (c t r u) -> p c t r u", c=PASSES, t=2, u=2
+            )
+            for t in range(2):
+                target = grouped_words[:, :, t, :, :]
+                source = turned_rows[n, t][:].rearrange("p c u r -> p c r u")
+                if n < PAIRS:
+                    nc.vector.tensor_copy(out=target, in_=source)
+                else:
+                    nc.scalar.copy(out=target, in_=source)
+            grouped_rows[n] = grouped
+
+        def quantise_rows(n):
+            nc.vector.quantize_mx(
+                out=row_pairs[n][1].bitcast(FP8X4), scales=row_pairs[n][2], in_=grouped_rows[n][:]
+            )
+
+        def row_tile_columns(tile_index, c):
+            first = (c * 2 + tile_index % 2) * P
+            return tile_index // 2, slice(first, first + P)
+
+        v_codes = keep.tile([P, PASSES, DV], U32, align_bytes=64)
+        v_scales = keep.tile([P, PASSES, DV], U8, align_bytes=64)
+        v_grouped = {}
+
+        def project(a):
+            half = a // 2
+            for g in range(PASSES):
+                if a % 2 == 0:
+                    v_grouped[g] = stream.tile(
+                        [P, BANK * PACK], BF16, name="v_grouped", align_bytes=64
+                    )
+                banks = []
+                for feature_tile in (2 * a, 2 * a + 1):
+                    v_bank = psum.tile([P, PACK, P], F32, tag="sum")
+                    for j in range(PACK):
+                        for c in range(PASSES):
+                            xa, x_cols = row_tile_columns(PACK * g + j, c)
+                            wa, w_cols = row_tile_columns(feature_tile, c)
+                            nc.tensor.matmul_mx(
+                                out=v_bank[:, j, :],
+                                lhsT=x3_codes[:, xa, x_cols].bitcast(FP8X4),
+                                lhsT_scale=x3_scales[:, xa, x_cols],
+                                rhs=wv_codes[:, wa, w_cols].bitcast(FP8X4),
+                                rhs_scale=wv_scales[:, wa, w_cols],
+                                start=(c == 0),
+                                stop=(c == PASSES - 1),
+                            )
+                    banks.append(v_bank)
+                for feature_tile, v_bank in zip((2 * a, 2 * a + 1), banks):
+                    first = (feature_tile % (BANK // P)) * P
+                    bias = bias_sb[:, feature_tile * P : (feature_tile + 1) * P]
+                    nc.vector.tensor_tensor(
+                        out=v_grouped[g][:].rearrange("p (n j) -> p n j", j=PACK)[
+                            :, first : first + P, :
+                        ],
+                        in0=v_bank[:].rearrange("p j n -> p n j"),
+                        in1=bias.unsqueeze(2).to_broadcast([P, P, PACK]),
+                        op=ALU.add,
+                    )
+                if a % 2 == 1:
+                    cols = slice(half * BANK, (half + 1) * BANK)
+                    nc.vector.quantize_mx(
+                        out=v_codes[:, g, cols].bitcast(FP8X4),
+                        scales=v_scales[:, g, cols],
+                        in_=v_grouped[g][:],
+                    )
+
+        def turn_features(rows_sb, name):
+            turned_sb = keep.tile([P, DK_HALVES * S], BF16, name=name)
+            turned_view = turned_sb[:].rearrange("p (h s) -> p h s", h=DK_HALVES)
+            for a in range(PAIRS):
+                turned = psum.tile([P, DK_HALVES, 2, P], BF16, tag="turn")
+                for h in range(DK_HALVES):
+                    for t in range(2):
+                        first = (2 * a + t) * DK + h * P
+                        nc.tensor.transpose(
+                            out=turned[:, h, t, :],
+                            in_=rows_sb[:, first : first + P],
+                            identity=ident_bf16[:],
+                        )
+                nc.scalar.copy(
+                    out=turned_view[:, :, 2 * a * P : 2 * (a + 1) * P],
+                    in_=turned[:].rearrange("p h t r -> p h (t r)"),
+                )
+            return turned_sb
+
+        transposed = {}
+        score_banks = {}
+        neg_z = {}
+        neg_max = {}
+        row_sum = {}
+        inv_sum = {}
+        weights = {}
+        turned_weights = {}
+        w_grouped = {}
+        w_codes = {}
+        w_scales = {}
+
+        def scores(i):
+            for n in range(S // BANK):
+                bank = psum.tile([P, BANK], F32, tag="wide", bufs=4)
+                for h in range(DK_HALVES):
+                    nc.tensor.matmul(
+                        out=bank[:],
+                        lhsT=transposed["q"][:, h * S + i * P : h * S + (i + 1) * P],
+                        rhs=transposed["k"][:, h * S + n * BANK : h * S + (n + 1) * BANK],
+                        start=(h == 0),
+                        stop=(h == DK_HALVES - 1),
+                    )
+                score_banks[i, n] = bank
+
+        def scale_and_maximum(i):
+            neg_z[i] = stream.tile([P, S], F32, name="neg_z")
+            for n in range(S // BANK):
+                cols = slice(n * BANK, (n + 1) * BANK)
+                nc.vector.tensor_tensor(
+                    out=neg_z[i][:, cols],
+                    in0=score_banks[i, n][:],
+                    in1=query_tile(recip, i)[:, cols],
+                    op=ALU.mult,
+                )
+            neg_max[i] = small.tile([P, 1], F32, name="neg_max")
+            nc.vector.tensor_reduce(out=neg_max[i][:], in_=neg_z[i][:], axis=AXIS.X, op=ALU.min)
+
+        def softmax_weights(i):
+            e = stream.tile([P, S], F32, bufs=3)
+            row_sum[i] = small.tile([P, 1], F32, name="row_sum")
+            nc.scalar.activation(
+                out=e[:],
+                in_=neg_z[i][:],
+                func=ACT.Exp,
+                bias=neg_max[i][:],
+                scale=-1.0,
+                accum_out=row_sum[i][:],
+            )
+            weights[i] = stream.tile([P, S], BF16, name="weights", bufs=4)
+            nc.gpsimd.tensor_tensor(
+                out=weights[i][:], in0=e[:], in1=query_tile(mask_sb, i), op=ALU.mult
+            )
+
+        def turn_weights(i):
+            words = weights[i][:].bitcast(F32)
+            turned = psum.tile([P, PASSES, 2, P], F32, tag="turn")
+            for g in range(PASSES):
+                for u in range(2):
+                    first = (g * 2 + u) * P
+                    nc.tensor.transpose(
+                        out=turned[:, g, u, :],
+                        in_=words[:, first : first + P],
+                        identity=ident_f32[:],
+                    )
+            w_grouped[i] = stream.tile([P, PASSES * P * PACK], BF16, name="w_grouped", align_bytes=64)
+            nc.scalar.copy(
+                out=w_grouped[i][:].bitcast(F32).rearrange("p (g r u) -> p g r u", g=PASSES, u=2),
+                in_=turned[:].rearrange("p g u r -> p g r u"),
+            )
+
+        def quantise_weights(i):
+            w_codes[i] = stream.tile([P, PASSES * P], U32, name="w_codes", align_bytes=64, bufs=3)
+            w_scales[i] = stream.tile([P, PASSES * P], U8, name="w_scales", align_bytes=64, bufs=3)
+            nc.vector.quantize_mx(
+                out=w_codes[i][:].bitcast(FP8X4), scales=w_scales[i][:], in_=w_grouped[i][:]
+            )
+            inv_sum[i] = small.tile([P, 1], F32, name="inv_sum")
+            nc.vector.reciprocal(out=inv_sum[i][:], in_=row_sum[i][:])
+
+        def output(i):
+            banks = []
+            for half in range(DV_HALVES):
+                cols = slice(half * BANK, (half + 1) * BANK)
+                acc = psum.tile([P, BANK], F32, tag="sum")
+                for g in range(PASSES):
+                    nc.tensor.matmul_mx(
+                        out=acc[:],
+                        lhsT=w_codes[i][:, g * P : (g + 1) * P].bitcast(FP8X4),
+                        lhsT_scale=w_scales[i][:, g * P : (g + 1) * P],
+                        rhs=v_codes[:, g, cols].bitcast(FP8X4),
+                        rhs_scale=v_scales[:, g, cols],
+                        start=(g == 0),
+                        stop=(g == PASSES - 1),
+                    )
+                banks.append(acc)
+            result = stream.tile([P, DV], F32)
+            for half in range(DV_HALVES):
+                cols = slice(half * BANK, (half + 1) * BANK)
+                nc.scalar.activation(
+                    out=result[:, cols], in_=banks[half][:], func=ACT.Copy, scale=inv_sum[i][:]
+                )
+            nc.sync.dma_start(out=out_rows[i], in_=result[:])
+
+        def reciprocal_steps_scalar(n):
+            if n < PAIRS:
+                logarithm(n)
+            elif n - PAIRS < TILES:
+                seed(n - PAIRS)
+
+        def reciprocal_steps_vector(n):
+            if 0 <= n - PAIRS - 2 < TILES:
+                newton(n - PAIRS - 2)
+
+        n_pairs = len(row_pairs)
+        front_rounds = n_pairs + 3
+        for n in range(front_rounds):
+            if n < n_pairs:
+                turn_rows(n)
+            if n == n_pairs:
+                transposed["k"] = turn_features(k_sb, "kT")
+            if n == n_pairs + 1:
+                transposed["q"] = turn_features(q_sb, "qT")
+            reciprocal_steps_scalar(n)
+            if 0 <= n - 1 < n_pairs:
+                gather_rows(n - 1)
+            if 0 <= n - 2 < n_pairs:
+                quantise_rows(n - 2)
+            if PAIRS <= n - 3 < n_pairs:
+                project(n - 3 - PAIRS)
+            reciprocal_steps_vector(n)
+
+        scores(0)
+        for s in range(TILES + 3):
+            if s + 1 < TILES:
+                scores(s + 1)
+            if 0 <= s - 2 < TILES:
+                turn_weights(s - 2)
+            if 0 <= s - 3 < TILES:
+                output(s - 3)
+            reciprocal_steps_scalar(front_rounds + s)
+            if s < TILES:
+                scale_and_maximum(s)
+            if 0 <= s - 2 < TILES:
+                quantise_weights(s - 2)
+            if s < TILES:
+                softmax_weights(s)
+            reciprocal_steps_vector(front_rounds + s)

@@ -106,7 +106,7 @@ def tile_model_pa_kernel(tc, q, k, x3, Wv, bv, inv_scale, dropout_mask, out):
             r = query_tile(recip, i)
             nc.scalar.activation(out=r, in_=r, func=ACT.Exp, scale=-1.0)
             x_times_seed[i] = stream.tile([P, S], F32, name="x_times_seed", bufs=4)
-            nc.gpsimd.tensor_tensor(
+            nc.vector.tensor_tensor(
                 out=x_times_seed[i][:], in0=query_tile(inv_sb, i), in1=r, op=ALU.mult
             )
 

@@ -95,19 +95,21 @@ def tile_model_pa_kernel(tc, q, k, x3, Wv, bv, inv_scale, dropout_mask, out):
             nc.tensor.matmul(out=spread[:], lhsT=ones[:], rhs=bias_row[:, cols], start=True, stop=True)
             nc.vector.tensor_copy(out=bias_sb[:, cols], in_=spread[:])
 
-        recip = []
+        recip = [keep.tile([P, 2 * S], F32, name="recip%d" % a) for a in range(PAIRS)]
         x_times_seed = {}
-
-        def logarithm(a):
-            recip.append(keep.tile([P, 2 * S], F32, name="recip%d" % a))
-            nc.scalar.activation(out=recip[a][:], in_=inv_sb[a][:], func=ACT.Ln)
 
         def seed(i):
             r = query_tile(recip, i)
-            nc.scalar.activation(out=r, in_=r, func=ACT.Exp, scale=-1.0)
-            x_times_seed[i] = stream.tile([P, S], F32, name="x_times_seed", bufs=4)
-            nc.vector.tensor_tensor(
-                out=x_times_seed[i][:], in0=query_tile(inv_sb, i), in1=r, op=ALU.mult
+            nc.scalar.activation(out=r, in_=query_tile(inv_sb, i), func=ACT.Abs_reciprocal_sqrt)
+            nc.scalar.activation(out=r, in_=r, func=ACT.Square)
+
+        def product(i):
+            x_times_seed[i] = stream.tile([P, S], F32, name="x_times_seed", bufs=1)
+            nc.gpsimd.tensor_tensor(
+                out=x_times_seed[i][:],
+                in0=query_tile(inv_sb, i),
+                in1=query_tile(recip, i),
+                op=ALU.mult,
             )
 
         def newton(i):
@@ -115,6 +117,11 @@ def tile_model_pa_kernel(tc, q, k, x3, Wv, bv, inv_scale, dropout_mask, out):
             nc.vector.scalar_tensor_tensor(
                 out=r, in0=x_times_seed[i][:], scalar=2.0, in1=r, op0=ALU.subtract, op1=ALU.mult
             )
+
+        def newton_then_product(i):
+            if i > 0:
+                newton(i - 1)
+            product(i)
 
         x3_codes = keep.tile([P, PAIRS, PAIR_COLS], U32, align_bytes=64)
         x3_scales = keep.tile([P, PAIRS, PAIR_COLS], U8, align_bytes=64)
@@ -168,7 +175,6 @@ def tile_model_pa_kernel(tc, q, k, x3, Wv, bv, inv_scale, dropout_mask, out):
         v_grouped = {}
 
         def project(a):
-            half = a // 2
             for g in range(PASSES):
                 if a % 2 == 0:
                     v_grouped[g] = stream.tile(
@@ -202,8 +208,9 @@ def tile_model_pa_kernel(tc, q, k, x3, Wv, bv, inv_scale, dropout_mask, out):
                         in1=bias.unsqueeze(2).to_broadcast([P, P, PACK]),
                         op=ALU.add,
                     )
-                if a % 2 == 1:
-                    cols = slice(half * BANK, (half + 1) * BANK)
+            if a % 2 == 1:
+                cols = slice((a // 2) * BANK, (a // 2 + 1) * BANK)
+                for g in range(PASSES):
                     nc.vector.quantize_mx(
                         out=v_codes[:, g, cols].bitcast(FP8X4),
                         scales=v_scales[:, g, cols],
@@ -333,33 +340,32 @@ def tile_model_pa_kernel(tc, q, k, x3, Wv, bv, inv_scale, dropout_mask, out):
                 )
             nc.sync.dma_start(out=out_rows[i], in_=result[:])
 
-        def reciprocal_steps_scalar(n):
-            if n < PAIRS:
-                logarithm(n)
-            elif n - PAIRS < TILES:
-                seed(n - PAIRS)
-
-        def reciprocal_steps_vector(n):
-            if 0 <= n - PAIRS - 2 < TILES:
-                newton(n - PAIRS - 2)
-
         n_pairs = len(row_pairs)
-        front_rounds = n_pairs + 3
-        for n in range(front_rounds):
+        first_projection = PAIRS + 3
+        early = TILES // 2
+        for n in range(n_pairs + 3):
             if n < n_pairs:
                 turn_rows(n)
             if n == n_pairs:
                 transposed["k"] = turn_features(k_sb, "kT")
             if n == n_pairs + 1:
                 transposed["q"] = turn_features(q_sb, "qT")
-            reciprocal_steps_scalar(n)
-            if 0 <= n - 1 < n_pairs:
-                gather_rows(n - 1)
+            if n < early // 2:
+                seed(2 * n)
+                seed(2 * n + 1)
+            if early <= early + n + 2 - first_projection < TILES:
+                seed(early + n + 2 - first_projection)
             if 0 <= n - 2 < n_pairs:
                 quantise_rows(n - 2)
-            if PAIRS <= n - 3 < n_pairs:
-                project(n - 3 - PAIRS)
-            reciprocal_steps_vector(n)
+            if 1 <= n <= early:
+                newton_then_product(n - 1)
+            if n >= first_projection:
+                newton_then_product(early + n - first_projection)
+            if 0 <= n - 1 < n_pairs:
+                gather_rows(n - 1)
+            if n >= first_projection:
+                project(n - first_projection)
+        newton(TILES - 1)
 
         scores(0)
         for s in range(TILES + 3):
@@ -369,11 +375,9 @@ def tile_model_pa_kernel(tc, q, k, x3, Wv, bv, inv_scale, dropout_mask, out):
                 turn_weights(s - 2)
             if 0 <= s - 3 < TILES:
                 output(s - 3)
-            reciprocal_steps_scalar(front_rounds + s)
             if s < TILES:
                 scale_and_maximum(s)
             if 0 <= s - 2 < TILES:
                 quantise_weights(s - 2)
             if s < TILES:
                 softmax_weights(s)
-            reciprocal_steps_vector(front_rounds + s)

@@ -28,6 +28,7 @@ PASSES = S // K_PASS
 DK_HALVES = DK // P
 DV_HALVES = DV // BANK
 PAIR_COLS = PASSES * 2 * P
+EARLY = TILES // 2
 
 FLOPS = 2 * S * D * DV + 2 * S * S * DK + 2 * S * S * DV
 
@@ -104,7 +105,7 @@ def tile_model_pa_kernel(tc, q, k, x3, Wv, bv, inv_scale, dropout_mask, out):
             nc.scalar.activation(out=r, in_=r, func=ACT.Square)
 
         def product(i):
-            x_times_seed[i] = stream.tile([P, S], F32, name="x_times_seed", bufs=1)
+            x_times_seed[i] = stream.tile([P, S], F32, name="x_times_seed", bufs=EARLY)
             nc.gpsimd.tensor_tensor(
                 out=x_times_seed[i][:],
                 in0=query_tile(inv_sb, i),
@@ -117,11 +118,6 @@ def tile_model_pa_kernel(tc, q, k, x3, Wv, bv, inv_scale, dropout_mask, out):
             nc.vector.scalar_tensor_tensor(
                 out=r, in0=x_times_seed[i][:], scalar=2.0, in1=r, op0=ALU.subtract, op1=ALU.mult
             )
-
-        def newton_then_product(i):
-            if i > 0:
-                newton(i - 1)
-            product(i)
 
         x3_codes = keep.tile([P, PAIRS, PAIR_COLS], U32, align_bytes=64)
         x3_scales = keep.tile([P, PAIRS, PAIR_COLS], U8, align_bytes=64)
@@ -182,7 +178,7 @@ def tile_model_pa_kernel(tc, q, k, x3, Wv, bv, inv_scale, dropout_mask, out):
                     )
                 banks = []
                 for feature_tile in (2 * a, 2 * a + 1):
-                    v_bank = psum.tile([P, PACK, P], F32, tag="sum")
+                    v_bank = psum.tile([P, PACK, P], F32, tag="sum" if g == 0 else "turn")
                     for j in range(PACK):
                         for c in range(PASSES):
                             xa, x_cols = row_tile_columns(PACK * g + j, c)
@@ -286,7 +282,8 @@ def tile_model_pa_kernel(tc, q, k, x3, Wv, bv, inv_scale, dropout_mask, out):
                 accum_out=row_sum[i][:],
             )
             weights[i] = stream.tile([P, S], BF16, name="weights", bufs=4)
-            nc.gpsimd.tensor_tensor(
+            engine = nc.gpsimd if i < TILES - 1 else nc.vector
+            engine.tensor_tensor(
                 out=weights[i][:], in0=e[:], in1=query_tile(mask_sb, i), op=ALU.mult
             )
 
@@ -342,30 +339,29 @@ def tile_model_pa_kernel(tc, q, k, x3, Wv, bv, inv_scale, dropout_mask, out):
 
         n_pairs = len(row_pairs)
         first_projection = PAIRS + 3
-        early = TILES // 2
         for n in range(n_pairs + 3):
+            a = n - first_projection
             if n < n_pairs:
                 turn_rows(n)
             if n == n_pairs:
                 transposed["k"] = turn_features(k_sb, "kT")
             if n == n_pairs + 1:
                 transposed["q"] = turn_features(q_sb, "qT")
-            if n < early // 2:
-                seed(2 * n)
-                seed(2 * n + 1)
-            if early <= early + n + 2 - first_projection < TILES:
-                seed(early + n + 2 - first_projection)
+            if n < EARLY // 2:
+                for i in (2 * n, 2 * n + 1):
+                    seed(i)
+                    product(i)
+            if 0 <= a + 1 < PAIRS:
+                seed(EARLY + a + 1)
             if 0 <= n - 2 < n_pairs:
                 quantise_rows(n - 2)
-            if 1 <= n <= early:
-                newton_then_product(n - 1)
-            if n >= first_projection:
-                newton_then_product(early + n - first_projection)
+            if a >= 0:
+                newton(a)
+                product(EARLY + a)
             if 0 <= n - 1 < n_pairs:
                 gather_rows(n - 1)
-            if n >= first_projection:
-                project(n - first_projection)
-        newton(TILES - 1)
+            if a >= 0:
+                project(a)
 
         scores(0)
         for s in range(TILES + 3):
@@ -379,5 +375,7 @@ def tile_model_pa_kernel(tc, q, k, x3, Wv, bv, inv_scale, dropout_mask, out):
                 scale_and_maximum(s)
             if 0 <= s - 2 < TILES:
                 quantise_weights(s - 2)
+            if EARLY + s < TILES:
+                newton(EARLY + s)
             if s < TILES:
                 softmax_weights(s)

@@ -28,7 +28,9 @@ PASSES = S // K_PASS
 DK_HALVES = DK // P
 DV_HALVES = DV // BANK
 PAIR_COLS = PASSES * 2 * P
-EARLY = TILES // 2
+LOADS = [("inv", 0), ("x3", 0), ("Wv", 0), ("inv", 1), ("x3", 1), ("Wv", 1), ("inv", 2), ("Wv", 2), ("Wv", 3), ("inv", 3), ("x3", 2), ("x3", 3), ("k", 0), ("q", 0)]
+ROW_PAIRS = [(w, a) for w, a in LOADS if w in ("x3", "Wv")]
+
 
 FLOPS = 2 * S * D * DV + 2 * S * S * DK + 2 * S * S * DV
 
@@ -53,28 +55,29 @@ def tile_model_pa_kernel(tc, q, k, x3, Wv, bv, inv_scale, dropout_mask, out):
         bias_row = keep.tile([P, DV], BF16)
         nc.vector.memset(bias_row[:].bitcast(I32), 0)
         nc.sync.dma_start(out=bias_row[0:1, :], in_=bv.rearrange("(o n) -> o n", o=1))
-        inv_sb = []
-        x3_sb = []
-        for a in range(PAIRS):
-            inv_sb.append(keep.tile([P, 2 * S], BF16, name="inv%d" % a))
-            nc.sync.dma_start(out=inv_sb[a][:], in_=inv_rows[a])
-            x3_sb.append(keep.tile([P, 2 * D], BF16, name="x3_%d" % a))
-            nc.sync.dma_start(out=x3_sb[a][:], in_=x3_rows[a])
-        wv_sb = []
-        for a in range(PAIRS):
-            wv_sb.append(keep.tile([P, 2 * D], BF16, name="wv_%d" % a))
-            nc.sync.dma_start(
-                out=wv_sb[a][:].rearrange("p (t d) -> p t d", t=2), in_=wv_rows[a]
-            )
+        inv_sb = [keep.tile([P, 2 * S], BF16, name="inv%d" % a) for a in range(PAIRS)]
+        x3_sb = [keep.tile([P, 2 * D], BF16, name="x3_%d" % a) for a in range(PAIRS)]
+        wv_sb = [keep.tile([P, 2 * D], BF16, name="wv_%d" % a) for a in range(PAIRS)]
         k_sb = keep.tile([P, TILES * DK], BF16)
-        nc.sync.dma_start(
-            out=k_sb[:].rearrange("p (t d) -> p t d", t=TILES),
-            in_=k.flatten_outer_dims().rearrange("(t p) d -> p t d", p=P),
-        )
         q_sb = keep.tile([P, TILES * DK], BF16)
-        nc.sync.dma_start(
-            out=q_sb[:], in_=q.flatten_outer_dims().rearrange("(p i) d -> p (i d)", i=TILES)
-        )
+        for what, a in LOADS:
+            if what == "inv":
+                nc.sync.dma_start(out=inv_sb[a][:], in_=inv_rows[a])
+            elif what == "x3":
+                nc.sync.dma_start(out=x3_sb[a][:], in_=x3_rows[a])
+            elif what == "Wv":
+                nc.sync.dma_start(
+                    out=wv_sb[a][:].rearrange("p (t d) -> p t d", t=2), in_=wv_rows[a]
+                )
+            elif what == "k":
+                nc.sync.dma_start(
+                    out=k_sb[:].rearrange("p (t d) -> p t d", t=TILES),
+                    in_=k.flatten_outer_dims().rearrange("(t p) d -> p t d", p=P),
+                )
+            else:
+                nc.sync.dma_start(
+                    out=q_sb[:], in_=q.flatten_outer_dims().rearrange("(p i) d -> p (i d)", i=TILES)
+                )
         mask_sb = []
         for a in range(PAIRS):
             mask_sb.append(keep.tile([P, 2 * S], BF16, name="mask%d" % a))
@@ -97,34 +100,23 @@ def tile_model_pa_kernel(tc, q, k, x3, Wv, bv, inv_scale, dropout_mask, out):
             nc.vector.tensor_copy(out=bias_sb[:, cols], in_=spread[:])
 
         recip = [keep.tile([P, 2 * S], F32, name="recip%d" % a) for a in range(PAIRS)]
-        x_times_seed = {}
 
-        def seed(i):
+        def logarithm(a):
+            nc.scalar.activation(out=recip[a][:], in_=inv_sb[a][:], func=ACT.Ln)
+
+        def reciprocal(i):
             r = query_tile(recip, i)
-            nc.scalar.activation(out=r, in_=query_tile(inv_sb, i), func=ACT.Abs_reciprocal_sqrt)
-            nc.scalar.activation(out=r, in_=r, func=ACT.Square)
-
-        def product(i):
-            x_times_seed[i] = stream.tile([P, S], F32, name="x_times_seed", bufs=EARLY)
-            nc.gpsimd.tensor_tensor(
-                out=x_times_seed[i][:],
-                in0=query_tile(inv_sb, i),
-                in1=query_tile(recip, i),
-                op=ALU.mult,
-            )
-
-        def newton(i):
-            r = query_tile(recip, i)
-            nc.vector.scalar_tensor_tensor(
-                out=r, in0=x_times_seed[i][:], scalar=2.0, in1=r, op0=ALU.subtract, op1=ALU.mult
-            )
+            nc.scalar.activation(out=r, in_=r, func=ACT.Exp, scale=-1.0)
 
         x3_codes = keep.tile([P, PAIRS, PAIR_COLS], U32, align_bytes=64)
         x3_scales = keep.tile([P, PAIRS, PAIR_COLS], U8, align_bytes=64)
         wv_codes = keep.tile([P, PAIRS, PAIR_COLS], U32, align_bytes=64)
         wv_scales = keep.tile([P, PAIRS, PAIR_COLS], U8, align_bytes=64)
-        row_pairs = [(x3_sb[a], x3_codes[:, a, :], x3_scales[:, a, :]) for a in range(PAIRS)] + [
-            (wv_sb[a], wv_codes[:, a, :], wv_scales[:, a, :]) for a in range(PAIRS)
+        row_pairs = [
+            (x3_sb[a], x3_codes[:, a, :], x3_scales[:, a, :])
+            if operand == "x3"
+            else (wv_sb[a], wv_codes[:, a, :], wv_scales[:, a, :])
+            for operand, a in ROW_PAIRS
         ]
         turned_rows = {}
         grouped_rows = {}
@@ -143,6 +135,9 @@ def tile_model_pa_kernel(tc, q, k, x3, Wv, bv, inv_scale, dropout_mask, out):
                         )
                 turned_rows[n, t] = turned
 
+        def on_vector(n, t):
+            return ROW_PAIRS[n][0] == "x3"
+
         def gather_rows(n):
             grouped = stream.tile([P, PAIR_COLS * PACK], BF16, align_bytes=64, bufs=3)
             grouped_words = grouped[:].bitcast(F32).rearrange(
@@ -151,7 +146,7 @@ def tile_model_pa_kernel(tc, q, k, x3, Wv, bv, inv_scale, dropout_mask, out):
             for t in range(2):
                 target = grouped_words[:, :, t, :, :]
                 source = turned_rows[n, t][:].rearrange("p c u r -> p c r u")
-                if n < PAIRS:
+                if on_vector(n, t):
                     nc.vector.tensor_copy(out=target, in_=source)
                 else:
                     nc.scalar.copy(out=target, in_=source)
@@ -169,49 +164,48 @@ def tile_model_pa_kernel(tc, q, k, x3, Wv, bv, inv_scale, dropout_mask, out):
         v_codes = keep.tile([P, PASSES, DV], U32, align_bytes=64)
         v_scales = keep.tile([P, PASSES, DV], U8, align_bytes=64)
         v_grouped = {}
+        v_banks = {}
 
-        def project(a):
-            for g in range(PASSES):
-                if a % 2 == 0:
-                    v_grouped[g] = stream.tile(
-                        [P, BANK * PACK], BF16, name="v_grouped", align_bytes=64
-                    )
-                banks = []
-                for feature_tile in (2 * a, 2 * a + 1):
-                    v_bank = psum.tile([P, PACK, P], F32, tag="sum" if g == 0 else "turn")
-                    for j in range(PACK):
-                        for c in range(PASSES):
-                            xa, x_cols = row_tile_columns(PACK * g + j, c)
-                            wa, w_cols = row_tile_columns(feature_tile, c)
-                            nc.tensor.matmul_mx(
-                                out=v_bank[:, j, :],
-                                lhsT=x3_codes[:, xa, x_cols].bitcast(FP8X4),
-                                lhsT_scale=x3_scales[:, xa, x_cols],
-                                rhs=wv_codes[:, wa, w_cols].bitcast(FP8X4),
-                                rhs_scale=wv_scales[:, wa, w_cols],
-                                start=(c == 0),
-                                stop=(c == PASSES - 1),
-                            )
-                    banks.append(v_bank)
-                for feature_tile, v_bank in zip((2 * a, 2 * a + 1), banks):
-                    first = (feature_tile % (BANK // P)) * P
-                    bias = bias_sb[:, feature_tile * P : (feature_tile + 1) * P]
-                    nc.vector.tensor_tensor(
-                        out=v_grouped[g][:].rearrange("p (n j) -> p n j", j=PACK)[
-                            :, first : first + P, :
-                        ],
-                        in0=v_bank[:].rearrange("p j n -> p n j"),
-                        in1=bias.unsqueeze(2).to_broadcast([P, P, PACK]),
-                        op=ALU.add,
-                    )
-            if a % 2 == 1:
-                cols = slice((a // 2) * BANK, (a // 2 + 1) * BANK)
-                for g in range(PASSES):
-                    nc.vector.quantize_mx(
-                        out=v_codes[:, g, cols].bitcast(FP8X4),
-                        scales=v_scales[:, g, cols],
-                        in_=v_grouped[g][:],
-                    )
+        def project(g, a):
+            for feature_tile in (2 * a, 2 * a + 1):
+                v_bank = psum.tile([P, PACK, P], F32, tag="sum" if (g + a) % 2 == 0 else "turn")
+                for j in range(PACK):
+                    for c in range(PASSES):
+                        xa, x_cols = row_tile_columns(PACK * g + j, c)
+                        wa, w_cols = row_tile_columns(feature_tile, c)
+                        nc.tensor.matmul_mx(
+                            out=v_bank[:, j, :],
+                            lhsT=x3_codes[:, xa, x_cols].bitcast(FP8X4),
+                            lhsT_scale=x3_scales[:, xa, x_cols],
+                            rhs=wv_codes[:, wa, w_cols].bitcast(FP8X4),
+                            rhs_scale=wv_scales[:, wa, w_cols],
+                            start=(c == 0),
+                            stop=(c == PASSES - 1),
+                        )
+                v_banks[g, feature_tile] = v_bank
+
+        def add_bias(g, a):
+            if a % 2 == 0:
+                v_grouped[g] = stream.tile([P, BANK * PACK], BF16, name="v_grouped", align_bytes=64)
+            for feature_tile in (2 * a, 2 * a + 1):
+                first = (feature_tile % (BANK // P)) * P
+                bias = bias_sb[:, feature_tile * P : (feature_tile + 1) * P]
+                nc.vector.tensor_tensor(
+                    out=v_grouped[g][:].rearrange("p (n j) -> p n j", j=PACK)[
+                        :, first : first + P, :
+                    ],
+                    in0=v_banks[g, feature_tile][:].rearrange("p j n -> p n j"),
+                    in1=bias.unsqueeze(2).to_broadcast([P, P, PACK]),
+                    op=ALU.add,
+                )
+
+        def quantise_values(g, half):
+            cols = slice(half * BANK, (half + 1) * BANK)
+            nc.vector.quantize_mx(
+                out=v_codes[:, g, cols].bitcast(FP8X4),
+                scales=v_scales[:, g, cols],
+                in_=v_grouped[g][:],
+            )
 
         def turn_features(rows_sb, name):
             turned_sb = keep.tile([P, DK_HALVES * S], BF16, name=name)
@@ -234,13 +228,15 @@ def tile_model_pa_kernel(tc, q, k, x3, Wv, bv, inv_scale, dropout_mask, out):
 
         transposed = {}
         score_banks = {}
-        neg_z = {}
+        z = {}
         neg_max = {}
         row_sum = {}
         inv_sum = {}
         weights = {}
+        exps = {}
         turned_weights = {}
         w_grouped = {}
+        out_banks = {}
         w_codes = {}
         w_scales = {}
 
@@ -257,34 +253,38 @@ def tile_model_pa_kernel(tc, q, k, x3, Wv, bv, inv_scale, dropout_mask, out):
                     )
                 score_banks[i, n] = bank
 
-        def scale_and_maximum(i):
-            neg_z[i] = stream.tile([P, S], F32, name="neg_z")
+        def scale(i):
+            z[i] = stream.tile([P, S], F32, name="z")
             for n in range(S // BANK):
                 cols = slice(n * BANK, (n + 1) * BANK)
                 nc.vector.tensor_tensor(
-                    out=neg_z[i][:, cols],
+                    out=z[i][:, cols],
                     in0=score_banks[i, n][:],
                     in1=query_tile(recip, i)[:, cols],
                     op=ALU.mult,
                 )
+
+        def maximum(i):
             neg_max[i] = small.tile([P, 1], F32, name="neg_max")
-            nc.vector.tensor_reduce(out=neg_max[i][:], in_=neg_z[i][:], axis=AXIS.X, op=ALU.min)
+            nc.vector.tensor_reduce(out=neg_max[i][:], in_=z[i][:], axis=AXIS.X, op=ALU.max, negate=True)
 
         def softmax_weights(i):
             e = stream.tile([P, S], F32, bufs=3)
             row_sum[i] = small.tile([P, 1], F32, name="row_sum")
             nc.scalar.activation(
                 out=e[:],
-                in_=neg_z[i][:],
+                in_=z[i][:],
                 func=ACT.Exp,
                 bias=neg_max[i][:],
-                scale=-1.0,
                 accum_out=row_sum[i][:],
             )
+            exps[i] = e
+
+        def mask_weights(i):
             weights[i] = stream.tile([P, S], BF16, name="weights", bufs=4)
             engine = nc.gpsimd if i < TILES - 1 else nc.vector
             engine.tensor_tensor(
-                out=weights[i][:], in0=e[:], in1=query_tile(mask_sb, i), op=ALU.mult
+                out=weights[i][:], in0=exps[i][:], in1=query_tile(mask_sb, i), op=ALU.mult
             )
 
         def turn_weights(i):
@@ -298,6 +298,10 @@ def tile_model_pa_kernel(tc, q, k, x3, Wv, bv, inv_scale, dropout_mask, out):
                         in_=words[:, first : first + P],
                         identity=ident_f32[:],
                     )
+            turned_weights[i] = turned
+
+        def copy_weights(i):
+            turned = turned_weights[i]
             w_grouped[i] = stream.tile([P, PASSES * P * PACK], BF16, name="w_grouped", align_bytes=64)
             nc.scalar.copy(
                 out=w_grouped[i][:].bitcast(F32).rearrange("p (g r u) -> p g r u", g=PASSES, u=2),
@@ -329,7 +333,11 @@ def tile_model_pa_kernel(tc, q, k, x3, Wv, bv, inv_scale, dropout_mask, out):
                         stop=(g == PASSES - 1),
                     )
                 banks.append(acc)
-            result = stream.tile([P, DV], F32)
+            out_banks[i] = banks
+
+        def finish(i):
+            banks = out_banks[i]
+            result = stream.tile([P, DV], F32, name="result", bufs=4)
             for half in range(DV_HALVES):
                 cols = slice(half * BANK, (half + 1) * BANK)
                 nc.scalar.activation(
@@ -337,45 +345,62 @@ def tile_model_pa_kernel(tc, q, k, x3, Wv, bv, inv_scale, dropout_mask, out):
                 )
             nc.sync.dma_start(out=out_rows[i], in_=result[:])
 
-        n_pairs = len(row_pairs)
-        first_projection = PAIRS + 3
+        n_pairs = len(ROW_PAIRS)
+        quantised = set()
+        open_projections = [(g, a) for g in range(PASSES) for a in range(PAIRS)]
+        ln_rounds = {0: [0], 2: [1], 4: [2], 6: [3]}
+        rc_rounds = {7: [0], 8: [1], 9: [2, 3, 4], 10: [5, 6, 7]}
         for n in range(n_pairs + 3):
-            a = n - first_projection
+            ready = [
+                (g, a)
+                for g, a in open_projections
+                if {("x3", 2 * g), ("x3", 2 * g + 1), ("Wv", a)} <= quantised
+            ][:1]
             if n < n_pairs:
                 turn_rows(n)
-            if n == n_pairs:
+            if n == 8:
                 transposed["k"] = turn_features(k_sb, "kT")
-            if n == n_pairs + 1:
+            if n == 9:
                 transposed["q"] = turn_features(q_sb, "qT")
-            if n < EARLY // 2:
-                for i in (2 * n, 2 * n + 1):
-                    seed(i)
-                    product(i)
-            if 0 <= a + 1 < PAIRS:
-                seed(EARLY + a + 1)
+            for g, a in ready:
+                project(g, a)
+                open_projections.remove((g, a))
+            for a in ln_rounds.get(n, []):
+                logarithm(a)
             if 0 <= n - 2 < n_pairs:
                 quantise_rows(n - 2)
-            if a >= 0:
-                newton(a)
-                product(EARLY + a)
+                quantised.add(ROW_PAIRS[n - 2])
             if 0 <= n - 1 < n_pairs:
                 gather_rows(n - 1)
-            if a >= 0:
-                project(a)
-
+            for i in rc_rounds.get(n, []):
+                reciprocal(i)
+            for g, a in ready:
+                add_bias(g, a)
+                if a % 2 == 1:
+                    quantise_values(g, a // 2)
         scores(0)
         for s in range(TILES + 3):
             if s + 1 < TILES:
                 scores(s + 1)
+            late = open_projections[:1]
+            for g, a in late:
+                project(g, a)
+                open_projections.remove((g, a))
             if 0 <= s - 2 < TILES:
                 turn_weights(s - 2)
+                copy_weights(s - 2)
             if 0 <= s - 3 < TILES:
                 output(s - 3)
+                finish(s - 3)
             if s < TILES:
-                scale_and_maximum(s)
+                scale(s)
+                maximum(s)
             if 0 <= s - 2 < TILES:
                 quantise_weights(s - 2)
-            if EARLY + s < TILES:
-                newton(EARLY + s)
             if s < TILES:
                 softmax_weights(s)
+                mask_weights(s)
+            for g, a in late:
+                add_bias(g, a)
+                if a % 2 == 1:
+                    quantise_values(g, a // 2)

@@ -345,6 +345,15 @@ def tile_model_pa_kernel(tc, q, k, x3, Wv, bv, inv_scale, dropout_mask, out):
                 )
             nc.sync.dma_start(out=out_rows[i], in_=result[:])
 
+        warm = psum.tile([P, BANK], F32, name="warm", tag="sum")
+
+        def keep_warm(count):
+            for product in range(count):
+                nc.tensor.matmul(
+                    out=warm[:], lhsT=ones[:], rhs=bias_row[:, 0:BANK], start=True, stop=True
+                )
+
+        keep_warm(2)
         n_pairs = len(ROW_PAIRS)
         quantised = set()
         open_projections = [(g, a) for g in range(PASSES) for a in range(PAIRS)]
@@ -358,6 +367,8 @@ def tile_model_pa_kernel(tc, q, k, x3, Wv, bv, inv_scale, dropout_mask, out):
             ][:1]
             if n < n_pairs:
                 turn_rows(n)
+            if n < 5:
+                keep_warm(2)
             if n == 8:
                 transposed["k"] = turn_features(k_sb, "kT")
             if n == 9:

@@ -28,9 +28,15 @@ PASSES = S // K_PASS
 DK_HALVES = DK // P
 DV_HALVES = DV // BANK
 PAIR_COLS = PASSES * 2 * P
-LOADS = [("inv", 0), ("x3", 0), ("Wv", 0), ("inv", 1), ("x3", 1), ("Wv", 1), ("inv", 2), ("Wv", 2), ("Wv", 3), ("inv", 3), ("x3", 2), ("x3", 3), ("k", 0), ("q", 0)]
-ROW_PAIRS = [(w, a) for w, a in LOADS if w in ("x3", "Wv")]
 
+LOADS = [
+    ("x3", 0), ("Wv", 0), ("bv", 0), ("inv", 0), ("Wv", 1), ("inv", 1), ("x3", 1), ("inv", 2),
+    ("Wv", 2), ("x3", 2), ("inv", 3), ("x3", 3), ("Wv", 3), ("k", 0), ("q", 0),
+]
+ROW_PAIRS = [(what, a) for what, a in LOADS if what in ("x3", "Wv")]
+VECTOR_PAIRS = 6
+
+MAXIMUM, EXPONENTS, MASKING, TURNING, GROUPING, QUANTISING, OUTPUT, FINISH = 1, 2, 2, 3, 4, 5, 6, 7
 
 FLOPS = 2 * S * D * DV + 2 * S * S * DK + 2 * S * S * DV
 
@@ -54,14 +60,15 @@ def tile_model_pa_kernel(tc, q, k, x3, Wv, bv, inv_scale, dropout_mask, out):
 
         bias_row = keep.tile([P, DV], BF16)
         nc.vector.memset(bias_row[:].bitcast(I32), 0)
-        nc.sync.dma_start(out=bias_row[0:1, :], in_=bv.rearrange("(o n) -> o n", o=1))
         inv_sb = [keep.tile([P, 2 * S], BF16, name="inv%d" % a) for a in range(PAIRS)]
         x3_sb = [keep.tile([P, 2 * D], BF16, name="x3_%d" % a) for a in range(PAIRS)]
         wv_sb = [keep.tile([P, 2 * D], BF16, name="wv_%d" % a) for a in range(PAIRS)]
         k_sb = keep.tile([P, TILES * DK], BF16)
         q_sb = keep.tile([P, TILES * DK], BF16)
         for what, a in LOADS:
-            if what == "inv":
+            if what == "bv":
+                nc.sync.dma_start(out=bias_row[0:1, :], in_=bv.rearrange("(o n) -> o n", o=1))
+            elif what == "inv":
                 nc.sync.dma_start(out=inv_sb[a][:], in_=inv_rows[a])
             elif what == "x3":
                 nc.sync.dma_start(out=x3_sb[a][:], in_=x3_rows[a])
@@ -90,19 +97,21 @@ def tile_model_pa_kernel(tc, q, k, x3, Wv, bv, inv_scale, dropout_mask, out):
         make_identity(nc, ident_f32[:])
         ident_bf16 = keep.tile([P, P], BF16)
         make_identity(nc, ident_bf16[:])
-        ones = keep.tile([P, P], BF16)
+        ones = keep.tile([P, BANK], BF16)
         nc.vector.memset(ones[:], 1.0)
         bias_sb = keep.tile([P, DV], BF16)
-        for half in range(DV_HALVES):
-            cols = slice(half * BANK, (half + 1) * BANK)
-            spread = psum.tile([P, BANK], F32, tag="turn")
-            nc.tensor.matmul(out=spread[:], lhsT=ones[:], rhs=bias_row[:, cols], start=True, stop=True)
-            nc.vector.tensor_copy(out=bias_sb[:, cols], in_=spread[:])
+
+        def spread_bias():
+            for half in range(DV_HALVES):
+                cols = slice(half * BANK, (half + 1) * BANK)
+                spread = psum.tile([P, BANK], F32, tag="turn")
+                nc.tensor.matmul(out=spread[:], lhsT=ones[:, 0:P], rhs=bias_row[:, cols], start=True, stop=True)
+                nc.vector.tensor_copy(out=bias_sb[:, cols], in_=spread[:])
 
         recip = [keep.tile([P, 2 * S], F32, name="recip%d" % a) for a in range(PAIRS)]
 
-        def logarithm(a):
-            nc.scalar.activation(out=recip[a][:], in_=inv_sb[a][:], func=ACT.Ln)
+        def logarithm(i):
+            nc.scalar.activation(out=query_tile(recip, i), in_=query_tile(inv_sb, i), func=ACT.Ln)
 
         def reciprocal(i):
             r = query_tile(recip, i)
@@ -135,9 +144,6 @@ def tile_model_pa_kernel(tc, q, k, x3, Wv, bv, inv_scale, dropout_mask, out):
                         )
                 turned_rows[n, t] = turned
 
-        def on_vector(n, t):
-            return ROW_PAIRS[n][0] == "x3"
-
         def gather_rows(n):
             grouped = stream.tile([P, PAIR_COLS * PACK], BF16, align_bytes=64, bufs=3)
             grouped_words = grouped[:].bitcast(F32).rearrange(
@@ -146,7 +152,7 @@ def tile_model_pa_kernel(tc, q, k, x3, Wv, bv, inv_scale, dropout_mask, out):
             for t in range(2):
                 target = grouped_words[:, :, t, :, :]
                 source = turned_rows[n, t][:].rearrange("p c u r -> p c r u")
-                if on_vector(n, t):
+                if n < VECTOR_PAIRS:
                     nc.vector.tensor_copy(out=target, in_=source)
                 else:
                     nc.scalar.copy(out=target, in_=source)
@@ -167,8 +173,9 @@ def tile_model_pa_kernel(tc, q, k, x3, Wv, bv, inv_scale, dropout_mask, out):
         v_banks = {}
 
         def project(g, a):
+            tag = "turn" if len(v_banks) // 2 % 2 == 0 else "sum"
             for feature_tile in (2 * a, 2 * a + 1):
-                v_bank = psum.tile([P, PACK, P], F32, tag="sum" if (g + a) % 2 == 0 else "turn")
+                v_bank = psum.tile([P, PACK, P], F32, tag=tag)
                 for j in range(PACK):
                     for c in range(PASSES):
                         xa, x_cols = row_tile_columns(PACK * g + j, c)
@@ -254,7 +261,7 @@ def tile_model_pa_kernel(tc, q, k, x3, Wv, bv, inv_scale, dropout_mask, out):
                 score_banks[i, n] = bank
 
         def scale(i):
-            z[i] = stream.tile([P, S], F32, name="z")
+            z[i] = stream.tile([P, S], F32, name="z", bufs=3)
             for n in range(S // BANK):
                 cols = slice(n * BANK, (n + 1) * BANK)
                 nc.vector.tensor_tensor(
@@ -268,9 +275,9 @@ def tile_model_pa_kernel(tc, q, k, x3, Wv, bv, inv_scale, dropout_mask, out):
             neg_max[i] = small.tile([P, 1], F32, name="neg_max")
             nc.vector.tensor_reduce(out=neg_max[i][:], in_=z[i][:], axis=AXIS.X, op=ALU.max, negate=True)
 
-        def softmax_weights(i):
+        def exponents(i):
             e = stream.tile([P, S], F32, bufs=3)
-            row_sum[i] = small.tile([P, 1], F32, name="row_sum")
+            row_sum[i] = small.tile([P, 1], F32, name="row_sum", bufs=TILES)
             nc.scalar.activation(
                 out=e[:],
                 in_=z[i][:],
@@ -281,7 +288,7 @@ def tile_model_pa_kernel(tc, q, k, x3, Wv, bv, inv_scale, dropout_mask, out):
             exps[i] = e
 
         def mask_weights(i):
-            weights[i] = stream.tile([P, S], BF16, name="weights", bufs=4)
+            weights[i] = stream.tile([P, S], BF16, name="weights", bufs=3)
             engine = nc.gpsimd if i < TILES - 1 else nc.vector
             engine.tensor_tensor(
                 out=weights[i][:], in0=exps[i][:], in1=query_tile(mask_sb, i), op=ALU.mult
@@ -289,36 +296,33 @@ def tile_model_pa_kernel(tc, q, k, x3, Wv, bv, inv_scale, dropout_mask, out):
 
         def turn_weights(i):
             words = weights[i][:].bitcast(F32)
-            turned = psum.tile([P, PASSES, 2, P], F32, tag="turn")
+            turned_weights[i] = psum.tile([P, PASSES, 2, P], F32, tag="turn", name="turned_w")
             for g in range(PASSES):
                 for u in range(2):
                     first = (g * 2 + u) * P
                     nc.tensor.transpose(
-                        out=turned[:, g, u, :],
+                        out=turned_weights[i][:, g, u, :],
                         in_=words[:, first : first + P],
                         identity=ident_f32[:],
                     )
-            turned_weights[i] = turned
 
-        def copy_weights(i):
-            turned = turned_weights[i]
+        def group_weights(i):
             w_grouped[i] = stream.tile([P, PASSES * P * PACK], BF16, name="w_grouped", align_bytes=64)
             nc.scalar.copy(
                 out=w_grouped[i][:].bitcast(F32).rearrange("p (g r u) -> p g r u", g=PASSES, u=2),
-                in_=turned[:].rearrange("p g u r -> p g r u"),
+                in_=turned_weights[i][:].rearrange("p g u r -> p g r u"),
             )
 
         def quantise_weights(i):
-            w_codes[i] = stream.tile([P, PASSES * P], U32, name="w_codes", align_bytes=64, bufs=3)
-            w_scales[i] = stream.tile([P, PASSES * P], U8, name="w_scales", align_bytes=64, bufs=3)
+            w_codes[i] = stream.tile([P, PASSES * P], U32, name="w_codes", align_bytes=64, bufs=4)
+            w_scales[i] = stream.tile([P, PASSES * P], U8, name="w_scales", align_bytes=64, bufs=4)
             nc.vector.quantize_mx(
                 out=w_codes[i][:].bitcast(FP8X4), scales=w_scales[i][:], in_=w_grouped[i][:]
             )
-            inv_sum[i] = small.tile([P, 1], F32, name="inv_sum")
+            inv_sum[i] = small.tile([P, 1], F32, name="inv_sum", bufs=TILES)
             nc.vector.reciprocal(out=inv_sum[i][:], in_=row_sum[i][:])
 
         def output(i):
-            banks = []
             for half in range(DV_HALVES):
                 cols = slice(half * BANK, (half + 1) * BANK)
                 acc = psum.tile([P, BANK], F32, tag="sum")
@@ -332,86 +336,83 @@ def tile_model_pa_kernel(tc, q, k, x3, Wv, bv, inv_scale, dropout_mask, out):
                         start=(g == 0),
                         stop=(g == PASSES - 1),
                     )
-                banks.append(acc)
-            out_banks[i] = banks
+                out_banks[i, half] = acc
 
         def finish(i):
-            banks = out_banks[i]
-            result = stream.tile([P, DV], F32, name="result", bufs=4)
             for half in range(DV_HALVES):
                 cols = slice(half * BANK, (half + 1) * BANK)
+                result = stream.tile([P, BANK], F32, bufs=8)
                 nc.scalar.activation(
-                    out=result[:, cols], in_=banks[half][:], func=ACT.Copy, scale=inv_sum[i][:]
+                    out=result[:], in_=out_banks[i, half][:], func=ACT.Copy, scale=inv_sum[i][:]
                 )
-            nc.sync.dma_start(out=out_rows[i], in_=result[:])
+                nc.sync.dma_start(out=out_rows[i][:, cols], in_=result[:])
 
         warm = psum.tile([P, BANK], F32, name="warm", tag="sum")
 
-        def keep_warm(count):
-            for product in range(count):
-                nc.tensor.matmul(
-                    out=warm[:], lhsT=ones[:], rhs=bias_row[:, 0:BANK], start=True, stop=True
-                )
+        def keep_warm():
+            nc.tensor.matmul(out=warm[:], lhsT=ones[:, 0:P], rhs=ones[:], start=True, stop=True)
 
-        keep_warm(2)
+        keep_warm()
+        keep_warm()
         n_pairs = len(ROW_PAIRS)
         quantised = set()
-        open_projections = [(g, a) for g in range(PASSES) for a in range(PAIRS)]
-        ln_rounds = {0: [0], 2: [1], 4: [2], 6: [3]}
-        rc_rounds = {7: [0], 8: [1], 9: [2, 3, 4], 10: [5, 6, 7]}
-        for n in range(n_pairs + 3):
+        projections = [(g, a) for g in range(PASSES) for a in range(PAIRS)]
+        for n in range(n_pairs + 6):
             ready = [
                 (g, a)
-                for g, a in open_projections
+                for g, a in projections
                 if {("x3", 2 * g), ("x3", 2 * g + 1), ("Wv", a)} <= quantised
             ][:1]
+            if 1 <= n <= n_pairs:
+                gather_rows(n - 1)
+            if n == 1:
+                spread_bias()
+            if n < 3:
+                keep_warm()
+            if 1 <= n <= n_pairs:
+                quantise_rows(n - 1)
+                quantised.add(ROW_PAIRS[n - 1])
+            if 1 <= n <= PAIRS:
+                logarithm(2 * n - 2)
+                logarithm(2 * n - 1)
+            for g, a in ready:
+                project(g, a)
+                projections.remove((g, a))
+            if n == n_pairs:
+                transposed["k"] = turn_features(k_sb, "kT")
+            if 0 <= n - 6 < TILES:
+                reciprocal(n - 6)
+            for g, a in ready:
+                add_bias(g, a)
+                if a % 2 == 1:
+                    quantise_values(g, a // 2)
             if n < n_pairs:
                 turn_rows(n)
-            if n < 5:
-                keep_warm(2)
-            if n == 8:
-                transposed["k"] = turn_features(k_sb, "kT")
-            if n == 9:
+            if n == n_pairs + 2:
                 transposed["q"] = turn_features(q_sb, "qT")
-            for g, a in ready:
-                project(g, a)
-                open_projections.remove((g, a))
-            for a in ln_rounds.get(n, []):
-                logarithm(a)
-            if 0 <= n - 2 < n_pairs:
-                quantise_rows(n - 2)
-                quantised.add(ROW_PAIRS[n - 2])
-            if 0 <= n - 1 < n_pairs:
-                gather_rows(n - 1)
-            for i in rc_rounds.get(n, []):
-                reciprocal(i)
-            for g, a in ready:
-                add_bias(g, a)
-                if a % 2 == 1:
-                    quantise_values(g, a // 2)
+
+        def tile_of(beat, lag):
+            return [beat - lag] if 0 <= beat - lag < TILES else []
+
         scores(0)
-        for s in range(TILES + 3):
-            if s + 1 < TILES:
-                scores(s + 1)
-            late = open_projections[:1]
-            for g, a in late:
-                project(g, a)
-                open_projections.remove((g, a))
-            if 0 <= s - 2 < TILES:
-                turn_weights(s - 2)
-                copy_weights(s - 2)
-            if 0 <= s - 3 < TILES:
-                output(s - 3)
-                finish(s - 3)
-            if s < TILES:
-                scale(s)
-                maximum(s)
-            if 0 <= s - 2 < TILES:
-                quantise_weights(s - 2)
-            if s < TILES:
-                softmax_weights(s)
-                mask_weights(s)
-            for g, a in late:
-                add_bias(g, a)
-                if a % 2 == 1:
-                    quantise_values(g, a // 2)
+        for s in range(TILES + FINISH):
+            for i in tile_of(s, QUANTISING):
+                quantise_weights(i)
+            for i in tile_of(s, MAXIMUM):
+                maximum(i)
+            for i in tile_of(s, FINISH):
+                finish(i)
+            for i in tile_of(s, OUTPUT):
+                output(i)
+            for i in tile_of(s, 0):
+                scale(i)
+            for i in tile_of(s, TURNING):
+                turn_weights(i)
+            for i in tile_of(s, -1):
+                scores(i)
+            for i in tile_of(s, GROUPING):
+                group_weights(i)
+            for i in tile_of(s, EXPONENTS):
+                exponents(i)
+            for i in tile_of(s, MASKING):
+                mask_weights(i)

@@ -30,13 +30,16 @@ DV_HALVES = DV // BANK
 PAIR_COLS = PASSES * 2 * P
 
 LOADS = [
-    ("x3", 0), ("Wv", 0), ("bv", 0), ("inv", 0), ("Wv", 1), ("inv", 1), ("x3", 1), ("inv", 2),
-    ("Wv", 2), ("x3", 2), ("inv", 3), ("x3", 3), ("Wv", 3), ("k", 0), ("q", 0),
+    ("x3", 0), ("Wv", 0), ("bv", 0), ("x3", 1), ("inv", 0), ("Wv", 1), ("Wv", 2), ("inv", 1),
+    ("x3", 2), ("Wv", 3), ("inv", 2), ("x3", 3), ("k", 0), ("q", 0), ("inv", 3),
 ]
 ROW_PAIRS = [(what, a) for what, a in LOADS if what in ("x3", "Wv")]
-VECTOR_PAIRS = 6
+VECTOR_PAIRS = 3
+FIRST_LOGARITHM = 2
+FIRST_RECIPROCAL = FIRST_LOGARITHM + TILES - 1
+EARLY = 5
 
-MAXIMUM, EXPONENTS, MASKING, TURNING, GROUPING, QUANTISING, OUTPUT, FINISH = 1, 2, 2, 3, 4, 5, 6, 7
+EXPONENTS, MASKING, TURNING, OUTPUT, FINISH = 1, 2, 3, 4, 5
 
 FLOPS = 2 * S * D * DV + 2 * S * S * DK + 2 * S * S * DV
 
@@ -152,7 +155,7 @@ def tile_model_pa_kernel(tc, q, k, x3, Wv, bv, inv_scale, dropout_mask, out):
             for t in range(2):
                 target = grouped_words[:, :, t, :, :]
                 source = turned_rows[n, t][:].rearrange("p c u r -> p c r u")
-                if n < VECTOR_PAIRS:
+                if n < VECTOR_PAIRS or t == 0:
                     nc.vector.tensor_copy(out=target, in_=source)
                 else:
                     nc.scalar.copy(out=target, in_=source)
@@ -338,21 +341,30 @@ def tile_model_pa_kernel(tc, q, k, x3, Wv, bv, inv_scale, dropout_mask, out):
                     )
                 out_banks[i, half] = acc
 
-        def finish(i):
+        def finish(i, vector_helps):
             for half in range(DV_HALVES):
                 cols = slice(half * BANK, (half + 1) * BANK)
                 result = stream.tile([P, BANK], F32, bufs=8)
-                nc.scalar.activation(
-                    out=result[:], in_=out_banks[i, half][:], func=ACT.Copy, scale=inv_sum[i][:]
-                )
+                if vector_helps and half == 1:
+                    nc.vector.tensor_scalar(
+                        out=result[:],
+                        in0=out_banks[i, half][:],
+                        scalar1=inv_sum[i][:],
+                        scalar2=None,
+                        op0=ALU.mult,
+                    )
+                else:
+                    nc.scalar.activation(
+                        out=result[:], in_=out_banks[i, half][:], func=ACT.Copy, scale=inv_sum[i][:]
+                    )
                 nc.sync.dma_start(out=out_rows[i][:, cols], in_=result[:])
 
         warm = psum.tile([P, BANK], F32, name="warm", tag="sum")
 
         def keep_warm():
-            nc.tensor.matmul(out=warm[:], lhsT=ones[:, 0:P], rhs=ones[:], start=True, stop=True)
+            for product in range(2):
+                nc.tensor.matmul(out=warm[:], lhsT=ones[:, 0:P], rhs=ones[:], start=True, stop=True)
 
-        keep_warm()
         keep_warm()
         n_pairs = len(ROW_PAIRS)
         quantised = set()
@@ -362,57 +374,58 @@ def tile_model_pa_kernel(tc, q, k, x3, Wv, bv, inv_scale, dropout_mask, out):
                 (g, a)
                 for g, a in projections
                 if {("x3", 2 * g), ("x3", 2 * g + 1), ("Wv", a)} <= quantised
-            ][:1]
+            ][:2]
+            if n < 5:
+                keep_warm()
             if 1 <= n <= n_pairs:
                 gather_rows(n - 1)
-            if n == 1:
-                spread_bias()
-            if n < 3:
-                keep_warm()
+            if 0 <= n - FIRST_LOGARITHM < TILES:
+                logarithm(n - FIRST_LOGARITHM)
+            if 0 <= n - FIRST_RECIPROCAL < EARLY:
+                reciprocal(n - FIRST_RECIPROCAL)
+            if n < n_pairs:
+                turn_rows(n)
+            if n == n_pairs:
+                transposed["k"] = turn_features(k_sb, "kT")
+            if n == n_pairs + 4:
+                transposed["q"] = turn_features(q_sb, "qT")
             if 1 <= n <= n_pairs:
                 quantise_rows(n - 1)
                 quantised.add(ROW_PAIRS[n - 1])
-            if 1 <= n <= PAIRS:
-                logarithm(2 * n - 2)
-                logarithm(2 * n - 1)
             for g, a in ready:
                 project(g, a)
                 projections.remove((g, a))
-            if n == n_pairs:
-                transposed["k"] = turn_features(k_sb, "kT")
-            if 0 <= n - 6 < TILES:
-                reciprocal(n - 6)
             for g, a in ready:
                 add_bias(g, a)
                 if a % 2 == 1:
                     quantise_values(g, a // 2)
-            if n < n_pairs:
-                turn_rows(n)
-            if n == n_pairs + 2:
-                transposed["q"] = turn_features(q_sb, "qT")
+            if n == 1:
+                spread_bias()
 
         def tile_of(beat, lag):
             return [beat - lag] if 0 <= beat - lag < TILES else []
 
         scores(0)
         for s in range(TILES + FINISH):
-            for i in tile_of(s, QUANTISING):
-                quantise_weights(i)
-            for i in tile_of(s, MAXIMUM):
-                maximum(i)
             for i in tile_of(s, FINISH):
-                finish(i)
-            for i in tile_of(s, OUTPUT):
-                output(i)
-            for i in tile_of(s, 0):
-                scale(i)
+                finish(i, vector_helps=s >= TILES)
             for i in tile_of(s, TURNING):
                 turn_weights(i)
             for i in tile_of(s, -1):
                 scores(i)
-            for i in tile_of(s, GROUPING):
+            for i in tile_of(s, TURNING):
                 group_weights(i)
-            for i in tile_of(s, EXPONENTS):
-                exponents(i)
             for i in tile_of(s, MASKING):
                 mask_weights(i)
+            for i in tile_of(s, OUTPUT):
+                output(i)
+            for i in tile_of(s, 0):
+                scale(i)
+            for i in tile_of(s, EXPONENTS):
+                exponents(i)
+            for i in tile_of(s, -EARLY):
+                reciprocal(i)
+            for i in tile_of(s, TURNING):
+                quantise_weights(i)
+            for i in tile_of(s, 0):
+                maximum(i)

@@ -30,14 +30,13 @@ DV_HALVES = DV // BANK
 PAIR_COLS = PASSES * 2 * P
 
 LOADS = [
-    ("x3", 0), ("Wv", 0), ("bv", 0), ("x3", 1), ("inv", 0), ("Wv", 1), ("Wv", 2), ("inv", 1),
-    ("x3", 2), ("Wv", 3), ("inv", 2), ("x3", 3), ("k", 0), ("q", 0), ("inv", 3),
+    ("x3", 0), ("Wv", 0), ("bv", 0), ("x3", 1), ("Wv", 1), ("Wv", 2), ("inv", 0), ("Wv", 3),
+    ("inv", 1), ("x3", 2), ("inv", 2), ("x3", 3), ("inv", 3), ("k", 0), ("q", 0),
 ]
 ROW_PAIRS = [(what, a) for what, a in LOADS if what in ("x3", "Wv")]
-VECTOR_PAIRS = 3
-FIRST_LOGARITHM = 2
-FIRST_RECIPROCAL = FIRST_LOGARITHM + TILES - 1
-EARLY = 5
+VECTOR_PAIRS = 1
+LOGARITHMS = {4: [0], 5: [1], 6: [2], 7: [3], 8: [4, 5], 9: [6, 7]}
+EARLY = 3
 
 EXPONENTS, MASKING, TURNING, OUTPUT, FINISH = 1, 2, 3, 4, 5
 
@@ -103,6 +102,8 @@ def tile_model_pa_kernel(tc, q, k, x3, Wv, bv, inv_scale, dropout_mask, out):
         ones = keep.tile([P, BANK], BF16)
         nc.vector.memset(ones[:], 1.0)
         bias_sb = keep.tile([P, DV], BF16)
+        first_table = keep.tile([P, 1], F32)
+        nc.scalar.activation(out=first_table[:], in_=ones[:, 0:1], func=ACT.Ln)
 
         def spread_bias():
             for half in range(DV_HALVES):
@@ -155,7 +156,7 @@ def tile_model_pa_kernel(tc, q, k, x3, Wv, bv, inv_scale, dropout_mask, out):
             for t in range(2):
                 target = grouped_words[:, :, t, :, :]
                 source = turned_rows[n, t][:].rearrange("p c u r -> p c r u")
-                if n < VECTOR_PAIRS or t == 0:
+                if n < VECTOR_PAIRS:
                     nc.vector.tensor_copy(out=target, in_=source)
                 else:
                     nc.scalar.copy(out=target, in_=source)
@@ -221,7 +222,7 @@ def tile_model_pa_kernel(tc, q, k, x3, Wv, bv, inv_scale, dropout_mask, out):
             turned_sb = keep.tile([P, DK_HALVES * S], BF16, name=name)
             turned_view = turned_sb[:].rearrange("p (h s) -> p h s", h=DK_HALVES)
             for a in range(PAIRS):
-                turned = psum.tile([P, DK_HALVES, 2, P], BF16, tag="turn")
+                turned = psum.tile([P, DK_HALVES, 2, P], BF16, tag="wide", bufs=4)
                 for h in range(DK_HALVES):
                     for t in range(2):
                         first = (2 * a + t) * DK + h * P
@@ -369,7 +370,7 @@ def tile_model_pa_kernel(tc, q, k, x3, Wv, bv, inv_scale, dropout_mask, out):
         n_pairs = len(ROW_PAIRS)
         quantised = set()
         projections = [(g, a) for g in range(PASSES) for a in range(PAIRS)]
-        for n in range(n_pairs + 6):
+        for n in range(n_pairs + 5):
             ready = [
                 (g, a)
                 for g, a in projections
@@ -379,22 +380,23 @@ def tile_model_pa_kernel(tc, q, k, x3, Wv, bv, inv_scale, dropout_mask, out):
                 keep_warm()
             if 1 <= n <= n_pairs:
                 gather_rows(n - 1)
-            if 0 <= n - FIRST_LOGARITHM < TILES:
-                logarithm(n - FIRST_LOGARITHM)
-            if 0 <= n - FIRST_RECIPROCAL < EARLY:
-                reciprocal(n - FIRST_RECIPROCAL)
+            for i in LOGARITHMS.get(n, []):
+                logarithm(i)
+            if n == n_pairs + 2:
+                for i in range(EARLY):
+                    reciprocal(i)
             if n < n_pairs:
                 turn_rows(n)
-            if n == n_pairs:
-                transposed["k"] = turn_features(k_sb, "kT")
-            if n == n_pairs + 4:
-                transposed["q"] = turn_features(q_sb, "qT")
             if 1 <= n <= n_pairs:
                 quantise_rows(n - 1)
                 quantised.add(ROW_PAIRS[n - 1])
             for g, a in ready:
                 project(g, a)
                 projections.remove((g, a))
+            if n == n_pairs:
+                transposed["k"] = turn_features(k_sb, "kT")
+            if n == n_pairs + 1:
+                transposed["q"] = turn_features(q_sb, "qT")
             for g, a in ready:
                 add_bias(g, a)
                 if a % 2 == 1:

from contextlib import ExitStack

import concourse.mybir as mybir
from concourse.masks import make_identity

F32 = mybir.dt.float32
BF16 = mybir.dt.bfloat16
I32 = mybir.dt.int32
U32 = mybir.dt.uint32
U8 = mybir.dt.uint8
FP8X4 = mybir.dt.float8_e4m3fn_x4
ALU = mybir.AluOpType
ACT = mybir.ActivationFunctionType
AXIS = mybir.AxisListType

P = 128
PACK = 4
K_PASS = P * PACK
S = 1024
D = 1024
DV = 1024
DK = 256
BANK = 512

TILES = S // P
PAIRS = TILES // 2
PASSES = S // K_PASS
DK_HALVES = DK // P
DV_HALVES = DV // BANK
PAIR_COLS = PASSES * 2 * P

LOADS = [
    ("x3", 0), ("Wv", 0), ("bv", 0), ("x3", 1), ("Wv", 1), ("Wv", 2), ("inv", 0), ("Wv", 3),
    ("inv", 1), ("x3", 2), ("inv", 2), ("x3", 3), ("inv", 3), ("k", 0), ("q", 0),
]
ROW_PAIRS = [(what, a) for what, a in LOADS if what in ("x3", "Wv")]
VECTOR_PAIRS = 1
LOGARITHMS = {4: [0], 5: [1], 6: [2], 7: [3], 8: [4, 5], 9: [6, 7]}
EARLY = 3

EXPONENTS, MASKING, TURNING, OUTPUT, FINISH = 1, 2, 3, 4, 5

FLOPS = 2 * S * D * DV + 2 * S * S * DK + 2 * S * S * DV


def tile_model_pa_kernel(tc, q, k, x3, Wv, bv, inv_scale, dropout_mask, out):
    nc = tc.nc
    with ExitStack() as ctx:
        ctx.enter_context(tc.manual_schedule())
        keep = ctx.enter_context(tc.tile_pool(name="keep", bufs=1))
        stream = ctx.enter_context(tc.tile_pool(name="stream", bufs=2))
        small = ctx.enter_context(tc.tile_pool(name="small", bufs=6))
        psum = ctx.enter_context(tc.psum_pool(name="psum", bufs=2))

        x3_rows = x3.flatten_outer_dims().rearrange("(a p e) d -> a p (e d)", p=P, e=2)
        wv_rows = Wv.rearrange("(a t p) d -> a p t d", t=2, p=P)
        inv_rows = inv_scale.rearrange("(p a i) n -> a p (i n)", a=PAIRS, i=2)
        mask_rows = dropout_mask.flatten_outer_dims().rearrange(
            "(p a i) n -> a p (i n)", a=PAIRS, i=2
        )
        out_rows = out.flatten_outer_dims().rearrange("(p i) n -> i p n", i=TILES)

        bias_row = keep.tile([P, DV], BF16)
        nc.vector.memset(bias_row[:].bitcast(I32), 0)
        inv_sb = [keep.tile([P, 2 * S], BF16, name="inv%d" % a) for a in range(PAIRS)]
        x3_sb = [keep.tile([P, 2 * D], BF16, name="x3_%d" % a) for a in range(PAIRS)]
        wv_sb = [keep.tile([P, 2 * D], BF16, name="wv_%d" % a) for a in range(PAIRS)]
        k_sb = keep.tile([P, TILES * DK], BF16)
        q_sb = keep.tile([P, TILES * DK], BF16)
        for what, a in LOADS:
            if what == "bv":
                nc.sync.dma_start(out=bias_row[0:1, :], in_=bv.rearrange("(o n) -> o n", o=1))
            elif what == "inv":
                nc.sync.dma_start(out=inv_sb[a][:], in_=inv_rows[a])
            elif what == "x3":
                nc.sync.dma_start(out=x3_sb[a][:], in_=x3_rows[a])
            elif what == "Wv":
                nc.sync.dma_start(
                    out=wv_sb[a][:].rearrange("p (t d) -> p t d", t=2), in_=wv_rows[a]
                )
            elif what == "k":
                nc.sync.dma_start(
                    out=k_sb[:].rearrange("p (t d) -> p t d", t=TILES),
                    in_=k.flatten_outer_dims().rearrange("(t p) d -> p t d", p=P),
                )
            else:
                nc.sync.dma_start(
                    out=q_sb[:], in_=q.flatten_outer_dims().rearrange("(p i) d -> p (i d)", i=TILES)
                )
        mask_sb = []
        for a in range(PAIRS):
            mask_sb.append(keep.tile([P, 2 * S], BF16, name="mask%d" % a))
            nc.sync.dma_start(out=mask_sb[a][:], in_=mask_rows[a])

        def query_tile(pair_list, i):
            return pair_list[i // 2][:, (i % 2) * S : (i % 2 + 1) * S]

        ident_f32 = keep.tile([P, P], F32)
        make_identity(nc, ident_f32[:])
        ident_bf16 = keep.tile([P, P], BF16)
        make_identity(nc, ident_bf16[:])
        ones = keep.tile([P, BANK], BF16)
        nc.vector.memset(ones[:], 1.0)
        bias_sb = keep.tile([P, DV], BF16)
        first_table = keep.tile([P, 1], F32)
        nc.scalar.activation(out=first_table[:], in_=ones[:, 0:1], func=ACT.Ln)

        def spread_bias():
            for half in range(DV_HALVES):
                cols = slice(half * BANK, (half + 1) * BANK)
                spread = psum.tile([P, BANK], F32, tag="turn")
                nc.tensor.matmul(out=spread[:], lhsT=ones[:, 0:P], rhs=bias_row[:, cols], start=True, stop=True)
                nc.vector.tensor_copy(out=bias_sb[:, cols], in_=spread[:])

        recip = [keep.tile([P, 2 * S], F32, name="recip%d" % a) for a in range(PAIRS)]

        def logarithm(i):
            nc.scalar.activation(out=query_tile(recip, i), in_=query_tile(inv_sb, i), func=ACT.Ln)

        def reciprocal(i):
            r = query_tile(recip, i)
            nc.scalar.activation(out=r, in_=r, func=ACT.Exp, scale=-1.0)

        x3_codes = keep.tile([P, PAIRS, PAIR_COLS], U32, align_bytes=64)
        x3_scales = keep.tile([P, PAIRS, PAIR_COLS], U8, align_bytes=64)
        wv_codes = keep.tile([P, PAIRS, PAIR_COLS], U32, align_bytes=64)
        wv_scales = keep.tile([P, PAIRS, PAIR_COLS], U8, align_bytes=64)
        row_pairs = [
            (x3_sb[a], x3_codes[:, a, :], x3_scales[:, a, :])
            if operand == "x3"
            else (wv_sb[a], wv_codes[:, a, :], wv_scales[:, a, :])
            for operand, a in ROW_PAIRS
        ]
        turned_rows = {}
        grouped_rows = {}

        def turn_rows(n):
            words = row_pairs[n][0][:].bitcast(F32)
            for t in range(2):
                turned = psum.tile([P, PASSES, 2, P], F32, tag="wide", bufs=4)
                for c in range(PASSES):
                    for u in range(2):
                        first = ((t * PASSES + c) * 2 + u) * P
                        nc.tensor.transpose(
                            out=turned[:, c, u, :],
                            in_=words[:, first : first + P],
                            identity=ident_f32[:],
                        )
                turned_rows[n, t] = turned

        def gather_rows(n):
            grouped = stream.tile([P, PAIR_COLS * PACK], BF16, align_bytes=64, bufs=3)
            grouped_words = grouped[:].bitcast(F32).rearrange(
                "p (c t r u) -> p c t r u", c=PASSES, t=2, u=2
            )
            for t in range(2):
                target = grouped_words[:, :, t, :, :]
                source = turned_rows[n, t][:].rearrange("p c u r -> p c r u")
                if n < VECTOR_PAIRS:
                    nc.vector.tensor_copy(out=target, in_=source)
                else:
                    nc.scalar.copy(out=target, in_=source)
            grouped_rows[n] = grouped

        def quantise_rows(n):
            nc.vector.quantize_mx(
                out=row_pairs[n][1].bitcast(FP8X4), scales=row_pairs[n][2], in_=grouped_rows[n][:]
            )

        def row_tile_columns(tile_index, c):
            first = (c * 2 + tile_index % 2) * P
            return tile_index // 2, slice(first, first + P)

        v_codes = keep.tile([P, PASSES, DV], U32, align_bytes=64)
        v_scales = keep.tile([P, PASSES, DV], U8, align_bytes=64)
        v_grouped = {}
        v_banks = {}

        def project(g, a):
            tag = "turn" if len(v_banks) // 2 % 2 == 0 else "sum"
            for feature_tile in (2 * a, 2 * a + 1):
                v_bank = psum.tile([P, PACK, P], F32, tag=tag)
                for j in range(PACK):
                    for c in range(PASSES):
                        xa, x_cols = row_tile_columns(PACK * g + j, c)
                        wa, w_cols = row_tile_columns(feature_tile, c)
                        nc.tensor.matmul_mx(
                            out=v_bank[:, j, :],
                            lhsT=x3_codes[:, xa, x_cols].bitcast(FP8X4),
                            lhsT_scale=x3_scales[:, xa, x_cols],
                            rhs=wv_codes[:, wa, w_cols].bitcast(FP8X4),
                            rhs_scale=wv_scales[:, wa, w_cols],
                            start=(c == 0),
                            stop=(c == PASSES - 1),
                        )
                v_banks[g, feature_tile] = v_bank

        def add_bias(g, a):
            if a % 2 == 0:
                v_grouped[g] = stream.tile([P, BANK * PACK], BF16, name="v_grouped", align_bytes=64)
            for feature_tile in (2 * a, 2 * a + 1):
                first = (feature_tile % (BANK // P)) * P
                bias = bias_sb[:, feature_tile * P : (feature_tile + 1) * P]
                nc.vector.tensor_tensor(
                    out=v_grouped[g][:].rearrange("p (n j) -> p n j", j=PACK)[
                        :, first : first + P, :
                    ],
                    in0=v_banks[g, feature_tile][:].rearrange("p j n -> p n j"),
                    in1=bias.unsqueeze(2).to_broadcast([P, P, PACK]),
                    op=ALU.add,
                )

        def quantise_values(g, half):
            cols = slice(half * BANK, (half + 1) * BANK)
            nc.vector.quantize_mx(
                out=v_codes[:, g, cols].bitcast(FP8X4),
                scales=v_scales[:, g, cols],
                in_=v_grouped[g][:],
            )

        def turn_features(rows_sb, name):
            turned_sb = keep.tile([P, DK_HALVES * S], BF16, name=name)
            turned_view = turned_sb[:].rearrange("p (h s) -> p h s", h=DK_HALVES)
            for a in range(PAIRS):
                turned = psum.tile([P, DK_HALVES, 2, P], BF16, tag="wide", bufs=4)
                for h in range(DK_HALVES):
                    for t in range(2):
                        first = (2 * a + t) * DK + h * P
                        nc.tensor.transpose(
                            out=turned[:, h, t, :],
                            in_=rows_sb[:, first : first + P],
                            identity=ident_bf16[:],
                        )
                nc.scalar.copy(
                    out=turned_view[:, :, 2 * a * P : 2 * (a + 1) * P],
                    in_=turned[:].rearrange("p h t r -> p h (t r)"),
                )
            return turned_sb

        transposed = {}
        score_banks = {}
        z = {}
        neg_max = {}
        row_sum = {}
        inv_sum = {}
        weights = {}
        exps = {}
        turned_weights = {}
        w_grouped = {}
        out_banks = {}
        w_codes = {}
        w_scales = {}

        def scores(i):
            for n in range(S // BANK):
                bank = psum.tile([P, BANK], F32, tag="wide", bufs=4)
                for h in range(DK_HALVES):
                    nc.tensor.matmul(
                        out=bank[:],
                        lhsT=transposed["q"][:, h * S + i * P : h * S + (i + 1) * P],
                        rhs=transposed["k"][:, h * S + n * BANK : h * S + (n + 1) * BANK],
                        start=(h == 0),
                        stop=(h == DK_HALVES - 1),
                    )
                score_banks[i, n] = bank

        def scale(i):
            z[i] = stream.tile([P, S], F32, name="z", bufs=3)
            for n in range(S // BANK):
                cols = slice(n * BANK, (n + 1) * BANK)
                nc.vector.tensor_tensor(
                    out=z[i][:, cols],
                    in0=score_banks[i, n][:],
                    in1=query_tile(recip, i)[:, cols],
                    op=ALU.mult,
                )

        def maximum(i):
            neg_max[i] = small.tile([P, 1], F32, name="neg_max")
            nc.vector.tensor_reduce(out=neg_max[i][:], in_=z[i][:], axis=AXIS.X, op=ALU.max, negate=True)

        def exponents(i):
            e = stream.tile([P, S], F32, bufs=3)
            row_sum[i] = small.tile([P, 1], F32, name="row_sum", bufs=TILES)
            nc.scalar.activation(
                out=e[:],
                in_=z[i][:],
                func=ACT.Exp,
                bias=neg_max[i][:],
                accum_out=row_sum[i][:],
            )
            exps[i] = e

        def mask_weights(i):
            weights[i] = stream.tile([P, S], BF16, name="weights", bufs=3)
            engine = nc.gpsimd if i < TILES - 1 else nc.vector
            engine.tensor_tensor(
                out=weights[i][:], in0=exps[i][:], in1=query_tile(mask_sb, i), op=ALU.mult
            )

        def turn_weights(i):
            words = weights[i][:].bitcast(F32)
            turned_weights[i] = psum.tile([P, PASSES, 2, P], F32, tag="turn", name="turned_w")
            for g in range(PASSES):
                for u in range(2):
                    first = (g * 2 + u) * P
                    nc.tensor.transpose(
                        out=turned_weights[i][:, g, u, :],
                        in_=words[:, first : first + P],
                        identity=ident_f32[:],
                    )

        def group_weights(i):
            w_grouped[i] = stream.tile([P, PASSES * P * PACK], BF16, name="w_grouped", align_bytes=64)
            nc.scalar.copy(
                out=w_grouped[i][:].bitcast(F32).rearrange("p (g r u) -> p g r u", g=PASSES, u=2),
                in_=turned_weights[i][:].rearrange("p g u r -> p g r u"),
            )

        def quantise_weights(i):
            w_codes[i] = stream.tile([P, PASSES * P], U32, name="w_codes", align_bytes=64, bufs=4)
            w_scales[i] = stream.tile([P, PASSES * P], U8, name="w_scales", align_bytes=64, bufs=4)
            nc.vector.quantize_mx(
                out=w_codes[i][:].bitcast(FP8X4), scales=w_scales[i][:], in_=w_grouped[i][:]
            )
            inv_sum[i] = small.tile([P, 1], F32, name="inv_sum", bufs=TILES)
            nc.vector.reciprocal(out=inv_sum[i][:], in_=row_sum[i][:])

        def output(i):
            for half in range(DV_HALVES):
                cols = slice(half * BANK, (half + 1) * BANK)
                acc = psum.tile([P, BANK], F32, tag="sum")
                for g in range(PASSES):
                    nc.tensor.matmul_mx(
                        out=acc[:],
                        lhsT=w_codes[i][:, g * P : (g + 1) * P].bitcast(FP8X4),
                        lhsT_scale=w_scales[i][:, g * P : (g + 1) * P],
                        rhs=v_codes[:, g, cols].bitcast(FP8X4),
                        rhs_scale=v_scales[:, g, cols],
                        start=(g == 0),
                        stop=(g == PASSES - 1),
                    )
                out_banks[i, half] = acc

        def finish(i, vector_helps):
            for half in range(DV_HALVES):
                cols = slice(half * BANK, (half + 1) * BANK)
                result = stream.tile([P, BANK], F32, bufs=8)
                if vector_helps and half == 1:
                    nc.vector.tensor_scalar(
                        out=result[:],
                        in0=out_banks[i, half][:],
                        scalar1=inv_sum[i][:],
                        scalar2=None,
                        op0=ALU.mult,
                    )
                else:
                    nc.scalar.activation(
                        out=result[:], in_=out_banks[i, half][:], func=ACT.Copy, scale=inv_sum[i][:]
                    )
                nc.sync.dma_start(out=out_rows[i][:, cols], in_=result[:])

        warm = psum.tile([P, BANK], F32, name="warm", tag="sum")

        def keep_warm():
            for product in range(2):
                nc.tensor.matmul(out=warm[:], lhsT=ones[:, 0:P], rhs=ones[:], start=True, stop=True)

        keep_warm()
        n_pairs = len(ROW_PAIRS)
        quantised = set()
        projections = [(g, a) for g in range(PASSES) for a in range(PAIRS)]
        for n in range(n_pairs + 5):
            ready = [
                (g, a)
                for g, a in projections
                if {("x3", 2 * g), ("x3", 2 * g + 1), ("Wv", a)} <= quantised
            ][:2]
            if n < 5:
                keep_warm()
            if 1 <= n <= n_pairs:
                gather_rows(n - 1)
            for i in LOGARITHMS.get(n, []):
                logarithm(i)
            if n == n_pairs + 2:
                for i in range(EARLY):
                    reciprocal(i)
            if n < n_pairs:
                turn_rows(n)
            if 1 <= n <= n_pairs:
                quantise_rows(n - 1)
                quantised.add(ROW_PAIRS[n - 1])
            for g, a in ready:
                project(g, a)
                projections.remove((g, a))
            if n == n_pairs:
                transposed["k"] = turn_features(k_sb, "kT")
            if n == n_pairs + 1:
                transposed["q"] = turn_features(q_sb, "qT")
            for g, a in ready:
                add_bias(g, a)
                if a % 2 == 1:
                    quantise_values(g, a // 2)
            if n == 1:
                spread_bias()

        def tile_of(beat, lag):
            return [beat - lag] if 0 <= beat - lag < TILES else []

        scores(0)
        for s in range(TILES + FINISH):
            for i in tile_of(s, FINISH):
                finish(i, vector_helps=s >= TILES)
            for i in tile_of(s, TURNING):
                turn_weights(i)
            for i in tile_of(s, -1):
                scores(i)
            for i in tile_of(s, TURNING):
                group_weights(i)
            for i in tile_of(s, MASKING):
                mask_weights(i)
            for i in tile_of(s, OUTPUT):
                output(i)
            for i in tile_of(s, 0):
                scale(i)
            for i in tile_of(s, EXPONENTS):
                exponents(i)
            for i in tile_of(s, -EARLY):
                reciprocal(i)
            for i in tile_of(s, TURNING):
                quantise_weights(i)
            for i in tile_of(s, 0):
                maximum(i)
